import numpy as np
import ml_dtypes


def mxq(x, axis, fmt="e4m3"):
    dtype, down = {"e4m3": (ml_dtypes.float8_e4m3fn, 7), "e5m2": (ml_dtypes.float8_e5m2, 14)}[fmt]
    v = np.moveaxis(np.asarray(x, np.float32).astype(ml_dtypes.bfloat16).astype(np.float64), axis, -1)
    blocks = v.reshape(v.shape[:-1] + (-1, 32))
    amax = np.abs(blocks).max(-1, keepdims=True)
    byte = np.maximum(np.where(amax > 0, np.frexp(amax)[1] - 1 + 127, 0) - down, 1)
    scale = np.exp2(byte - 127.0)
    codes = (blocks / scale).astype(np.float32).astype(dtype).astype(np.float64)
    return np.moveaxis((codes * scale).reshape(v.shape), -1, axis)


WIDE = False


def mx_kscale(k):
    if not WIDE:
        return np.ones(k)
    levels = np.array([30, -30])
    if k % 512:
        return np.exp2(np.random.permutation(np.resize(levels, k // 32))).repeat(32)
    a = np.empty((k // 512, 16))
    for p in range(k // 512):
        a[p, :8] = np.random.permutation(np.resize(levels, 8))
        for g in range(8):
            far = levels[np.abs(levels - a[p, g]) >= 10]
            a[p, g + 8] = far[np.random.randint(len(far))]
    return np.exp2(a.ravel()).repeat(32)


BF16 = ml_dtypes.bfloat16


def bf(x):
    return np.asarray(x, np.float32).astype(BF16)


def f64(x):
    return np.asarray(x).astype(np.float64)


B, N, D, E, H = 4, 128, 2048, 2048, 16
DH = E // H
ROPE_BASE = 10000.0


def rope_cos_sin():
    inv_freq = 1.0 / ROPE_BASE ** (np.arange(0, DH, 2) / DH)
    freqs = np.repeat(np.arange(N)[:, None] * inv_freq[None, :], 2, axis=-1)
    return np.cos(freqs), np.sin(freqs)


def rotate_half(v):
    p = v.reshape(v.shape[:-1] + (v.shape[-1] // 2, 2))
    return np.stack((-p[..., 1], p[..., 0]), axis=-1).reshape(v.shape)


def setup_inputs():
    s = mx_kscale(D)
    return {"x": bf(np.random.standard_normal((B, N, D)) * s),
            "Wq": bf(np.random.standard_normal((D, E)) * 3.0 / np.sqrt(D) / s[:, None]),
            "bq": bf(np.random.standard_normal(E) * 0.5),
            "Wk": bf(np.random.standard_normal((D, E)) * 3.0 / np.sqrt(D) / s[:, None]),
            "bk": bf(np.random.standard_normal(E) * 0.5)}


def reference(x, Wq, bq, Wk, bk):
    xq = mxq(f64(x), 2, "e5m2")
    q = ((xq @ mxq(f64(Wq), 0, "e5m2")) + f64(bq)).reshape(B, N, H, DH).transpose(0, 2, 1, 3)
    k = ((xq @ mxq(f64(Wk), 0, "e5m2")) + f64(bk)).reshape(B, N, H, DH).transpose(0, 2, 1, 3)
    cos, sin = rope_cos_sin()
    q = q * cos + rotate_half(q) * sin
    k = k * cos + rotate_half(k) * sin
    q = q * (1.0 / np.sqrt(DH))
    return q, k

@@ -1,0 +1,268 @@
+import math
+from contextlib import ExitStack
+
+import concourse.mybir as mybir
+from concourse.masks import make_identity
+
+F32 = mybir.dt.float32
+BF16 = mybir.dt.bfloat16
+U32 = mybir.dt.uint32
+U8 = mybir.dt.uint8
+I32 = mybir.dt.int32
+FP8X4 = mybir.dt.float8_e5m2_x4
+ALU = mybir.AluOpType
+ACT = mybir.ActivationFunctionType
+
+FLOPS = 2 * 512 * 2048 * 4096
+
+P = 128
+PASSES = 4
+KP = 512
+TOK = 512
+GC = 512
+NG = 8
+RAW_BUFS = 10
+V_HALVES = (1, 5, 7)
+
+TWO_PI = 2.0 * math.pi
+C1 = 6.28125
+C2 = TWO_PI - C1
+RATIO = 10000.0 ** (-1.0 / 64.0)
+
+
+def tile_attention_pa_kernel(tc, x, Wq, bq, Wk, bk, out_0, out_1):
+    nc = tc.nc
+    with ExitStack() as ctx:
+        const = ctx.enter_context(tc.tile_pool(name="const", bufs=1))
+        xin = ctx.enter_context(tc.tile_pool(name="xin", bufs=4))
+        xgp = ctx.enter_context(tc.tile_pool(name="xgp", bufs=4))
+        rawp = ctx.enter_context(tc.tile_pool(name="rawp", bufs=RAW_BUFS))
+        grp = ctx.enter_context(tc.tile_pool(name="grp", bufs=4))
+        codes = ctx.enter_context(tc.tile_pool(name="codes", bufs=3))
+        up = ctx.enter_context(tc.tile_pool(name="up", bufs=2))
+        op = ctx.enter_context(tc.tile_pool(name="op", bufs=6))
+        accp = ctx.enter_context(tc.psum_pool(name="accp", bufs=4))
+        trp = ctx.enter_context(tc.psum_pool(name="trp", bufs=4))
+
+        zero1 = const.tile([P, 1], F32, name="zero1", tag="zero1")
+        nc.vector.memset(zero1[:], 0.0)
+        warm = const.tile([P, 1], F32, name="warm", tag="warm")
+        nc.scalar.activation(out=warm[:], in_=zero1[:], func=ACT.Sin)
+
+        x_view = x.flatten_outer_dims().rearrange("(q j) k -> q j k", j=4)
+        units = [(G, g) for G in range(NG) for g in range(PASSES)]
+        raw_tiles = {}
+        x_tiles = {}
+
+        def load_x(g):
+            t = xin.tile([P, 4, KP], BF16, name="x_raw", tag="x_raw")
+            nc.sync.dma_start(out=t[:], in_=x_view[:, :, g * KP : (g + 1) * KP])
+            x_tiles[g] = t
+
+        def load_w(u):
+            G, g = units[u]
+            w = Wq if G < 4 else Wk
+            c0 = (G % 4) * GC
+            t = rawp.tile([P, 4, GC], BF16, name="w_raw", tag="w_raw")
+            nc.sync.dma_start(
+                out=t[:],
+                in_=w[g * KP : (g + 1) * KP, c0 : c0 + GC].rearrange("(p t) c -> p t c", t=4),
+            )
+            raw_tiles[u] = t
+
+        bias_rows = const.tile([32, P], BF16, name="bias_rows", tag="bias_rows")
+        nc.scalar.dma_start(out=bias_rows[0:16, :], in_=bq.rearrange("(m d) -> m d", d=P))
+        nc.scalar.dma_start(out=bias_rows[16:32, :], in_=bk.rearrange("(m d) -> m d", d=P))
+
+        for g in range(PASSES):
+            load_x(g)
+            load_w(g)
+        for u in range(PASSES, RAW_BUFS):
+            load_w(u)
+        next_load = [RAW_BUFS]
+
+        ident = const.tile([P, P], F32, name="ident", tag="ident")
+        make_identity(nc, ident[:])
+        pswap = const.tile([P, P], F32, name="pswap", tag="pswap")
+        ident_v = ident[:].rearrange("p (i e) -> p i e", e=2)
+        pswap_v = pswap[:].rearrange("p (i e) -> p i e", e=2)
+        nc.gpsimd.tensor_copy(out=pswap_v[:, :, 0], in_=ident_v[:, :, 1])
+        nc.gpsimd.tensor_copy(out=pswap_v[:, :, 1], in_=ident_v[:, :, 0])
+        pos = const.tile([P, P], F32, name="pos", tag="pos")
+        nc.gpsimd.iota(
+            pos[:], pattern=[[1, 4], [4, 32]], base=0, channel_multiplier=0,
+            allow_small_or_imprecise_dtypes=True,
+        )
+
+        rows = const.tile([P, 2, P], F32, name="rows", tag="rows")
+        nc.vector.memset(rows[:, 0, 0:2], 1.0)
+        for k in range(6):
+            w = 2 << k
+            nc.vector.tensor_scalar(
+                out=rows[:, 0, w : 2 * w], in0=rows[:, 0, 0:w], scalar1=RATIO ** (1 << k), scalar2=None,
+                op0=ALU.mult,
+            )
+        sign_v = rows[:, 1, :].rearrange("p (i e) -> p i e", e=2)
+        nc.vector.memset(sign_v[:, :, 0], 1.0)
+        nc.vector.memset(sign_v[:, :, 1], -1.0)
+        cols_ps = accp.tile([P, 512], F32, name="cols_ps", tag="acc")
+        nc.tensor.transpose(cols_ps[:, 0:P], rows[:, 0, :], ident[:])
+        nc.tensor.transpose(cols_ps[:, P : 2 * P], rows[:, 1, :], ident[:])
+        freq = const.tile([P, 1], F32, name="freq", tag="freq")
+        sign = const.tile([P, 1], F32, name="sign", tag="sign")
+        nc.vector.tensor_copy(out=freq[:], in_=cols_ps[:, 0:1])
+        nc.vector.tensor_copy(out=sign[:], in_=cols_ps[:, P : P + 1])
+
+        bias_sq = const.tile([P, P], F32, name="bias_sq", tag="bias_sq")
+        nc.vector.memset(bias_sq[:], 0.0)
+        nc.vector.tensor_copy(out=bias_sq[0:32, :], in_=bias_rows[:])
+        bias_ps = accp.tile([P, 512], F32, name="bias_ps", tag="acc")
+        nc.tensor.transpose(bias_ps[:, 0:P], bias_sq[:], ident[:])
+        bias = const.tile([P, 32], F32, name="bias", tag="bias")
+        nc.vector.tensor_copy(out=bias[:], in_=bias_ps[:, 0:32])
+
+        ang = const.tile([P, 2, P], F32, name="ang", tag="ang")
+        nc.vector.tensor_scalar(
+            out=ang[:, 0, :], in0=pos[:], scalar1=freq[:], scalar2=None, op0=ALU.mult
+        )
+        nc.vector.tensor_scalar(
+            out=ang[:, 1, :], in0=pos[:], scalar1=freq[:], scalar2=0.5 * math.pi, op0=ALU.mult, op1=ALU.add
+        )
+        ang_f = ang[:].rearrange("p a n -> p (a n)")
+        turns = const.tile([P, 2 * P], I32, name="turns", tag="turns")
+        nc.vector.tensor_scalar(
+            out=turns[:], in0=ang_f, scalar1=1.0 / TWO_PI, scalar2=None, op0=ALU.mult
+        )
+        red1 = const.tile([P, 2 * P], F32, name="red1", tag="red1")
+        nc.vector.scalar_tensor_tensor(
+            out=red1[:], in0=turns[:], scalar=-C1, in1=ang_f, op0=ALU.mult, op1=ALU.add
+        )
+        red2 = const.tile([P, 2 * P], F32, name="red2", tag="red2")
+        nc.vector.scalar_tensor_tensor(
+            out=red2[:], in0=turns[:], scalar=-C2, in1=red1[:], op0=ALU.mult, op1=ALU.add
+        )
+        over = const.tile([P, 2 * P], F32, name="over", tag="over")
+        nc.vector.tensor_scalar(out=over[:], in0=red2[:], scalar1=math.pi, scalar2=None, op0=ALU.is_gt)
+        red3 = const.tile([P, 2, 4, 32], F32, name="red3", tag="red3")
+        nc.vector.scalar_tensor_tensor(
+            out=red3[:].rearrange("p a j r -> p (a j r)"), in0=over[:], scalar=-TWO_PI, in1=red2[:],
+            op0=ALU.mult, op1=ALU.add,
+        )
+        cos_t = const.tile([P, 4, 4, 32], F32, name="cos_t", tag="cos_t")
+        sin_t = const.tile([P, 4, 4, 32], F32, name="sin_t", tag="sin_t")
+        for b in range(4):
+            nc.scalar.activation(out=sin_t[:, :, b, :], in_=red3[:, 0, :, :], func=ACT.Sin, scale=sign[:])
+            nc.scalar.activation(out=cos_t[:, :, b, :], in_=red3[:, 1, :, :], func=ACT.Sin)
+        cos_v = cos_t[:].rearrange("p j b r -> p (j b) r")
+        sin_v = sin_t[:].rearrange("p j b r -> p (j b) r")
+
+        xc = const.tile([P, PASSES, TOK], U32, name="xc", tag="xc", align_bytes=64)
+        xs = const.tile([P, PASSES, TOK], U8, name="xs", tag="xs", align_bytes=64)
+
+        def prep_x(g):
+            xg = xgp.tile([P, TOK, 4], BF16, name="xg", tag="xg", align_bytes=64)
+            xg_w = xg[:].rearrange("p c t -> p (c t)").bitcast(F32)
+            for jp in range(2):
+                xt = trp.tile([P, 512], F32, name="xt", tag="tr")
+                xt_v = xt[:].rearrange("p (jj u q) -> p jj u q", jj=2, u=2)
+                for jj in range(2):
+                    words = x_tiles[g][:, 2 * jp + jj, :].bitcast(F32)
+                    for u in range(2):
+                        nc.tensor.transpose(xt_v[:, jj, u, :], words[:, u:256:2], ident[:])
+                dst = xg_w[:, jp * 512 : (jp + 1) * 512].rearrange("p (jj q u) -> p jj q u", jj=2, u=2)
+                src = xt[:].rearrange("p (jj u q) -> p jj q u", jj=2, u=2)
+                if jp == 0:
+                    nc.vector.tensor_copy(out=dst, in_=src)
+                else:
+                    nc.scalar.copy(out=dst, in_=src)
+            nc.vector.quantize_mx(
+                out=xc[:, g, :].bitcast(FP8X4), scales=xs[:, g, :], in_=xg[:].rearrange("p c t -> p (c t)")
+            )
+
+        w_codes = {}
+        grouped = {}
+
+        def interleave(u):
+            G, g = units[u]
+            raw = raw_tiles.pop(u)
+            gt = grp.tile([P, GC, 4], BF16, name="w_grouped", tag="w_grouped", align_bytes=64)
+            for half in range(2):
+                cs = slice(half * 256, (half + 1) * 256)
+                src = raw[:, :, cs].rearrange("p t c -> p c t")
+                if 2 * g + half in V_HALVES:
+                    nc.vector.tensor_copy(out=gt[:, cs, :], in_=src)
+                else:
+                    nc.scalar.copy(out=gt[:, cs, :], in_=src)
+            grouped[u] = gt
+            if next_load[0] < len(units):
+                load_w(next_load[0])
+                next_load[0] += 1
+
+        def quantize(u):
+            G, g = units[u]
+            if g == 0:
+                wc_new = codes.tile([P, PASSES, GC], U32, name="wc", tag="wc", align_bytes=64)
+                ws_new = codes.tile([P, PASSES, GC], U8, name="ws", tag="ws", align_bytes=64)
+                w_codes[G] = (wc_new, ws_new)
+            wc, ws = w_codes[G]
+            gt = grouped.pop(u)
+            nc.vector.quantize_mx(
+                out=wc[:, g, :].bitcast(FP8X4), scales=ws[:, g, :], in_=gt[:].rearrange("p c t -> p (c t)")
+            )
+
+        for g in range(PASSES):
+            prep_x(g)
+            interleave(g)
+            quantize(g)
+
+        for G in range(NG):
+            wc, ws = w_codes.pop(G)
+            u1 = up.tile([P, 16, 4, 32], F32, name="u1", tag="u1")
+            u2 = up.tile([P, 16, 4, 32], F32, name="u2", tag="u2")
+            for h in range(4):
+                hc = slice(h * P, (h + 1) * P)
+                acc = accp.tile([P, 512], F32, name="acc", tag="acc")
+                for g in range(PASSES):
+                    nc.tensor.matmul_mx(
+                        out=acc[:],
+                        lhsT=wc[:, g, hc].bitcast(FP8X4),
+                        lhsT_scale=ws[:, g, hc],
+                        rhs=xc[:, g, :].bitcast(FP8X4),
+                        rhs_scale=xs[:, g, :],
+                        start=(g == 0),
+                        stop=(g == PASSES - 1),
+                    )
+                if G + 1 < NG:
+                    interleave(4 * (G + 1) + h)
+                acc_v = acc[:].rearrange("p (a r) -> p a r", r=32)
+                m = 4 * G + h
+                nc.vector.scalar_tensor_tensor(
+                    out=u1[:, :, h, :], in0=acc_v, scalar=bias[:, m : m + 1], in1=cos_v,
+                    op0=ALU.add, op1=ALU.mult,
+                )
+                nc.vector.scalar_tensor_tensor(
+                    out=u2[:, :, h, :], in0=acc_v, scalar=bias[:, m : m + 1], in1=sin_v,
+                    op0=ALU.add, op1=ALU.mult,
+                )
+                if G + 1 < NG:
+                    quantize(4 * (G + 1) + h)
+            out_m = out_0 if G < 4 else out_1
+            scale = 1.0 / math.sqrt(128.0) if G < 4 else 1.0
+            h0 = (G % 4) * 4
+            for b in range(4):
+                tr = trp.tile([P, 512], F32, name="tr", tag="tr")
+                for j in range(4):
+                    a = 4 * j + b
+                    nc.tensor.matmul(
+                        out=tr[:, j * P : (j + 1) * P], lhsT=u1[:, a, :, :].rearrange("p h r -> p (h r)"),
+                        rhs=ident[:], start=True, stop=False, is_transpose=True,
+                    )
+                    nc.tensor.matmul(
+                        out=tr[:, j * P : (j + 1) * P], lhsT=u2[:, a, :, :].rearrange("p h r -> p (h r)"),
+                        rhs=pswap[:], start=False, stop=True, is_transpose=True,
+                    )
+                o = op.tile([P, 512], F32, name="o", tag="o")
+                nc.scalar.activation(out=o[:], in_=tr[:], func=ACT.Copy, scale=scale)
+                nc.sync.dma_start(
+                    out=out_m[b, h0 : h0 + 4, :, :].rearrange("h (r j) d -> (h r) (j d)", j=4), in_=o[:]
+                )

@@ -12,6 +12,7 @@ I32 = mybir.dt.int32
 FP8X4 = mybir.dt.float8_e5m2_x4
 ALU = mybir.AluOpType
 ACT = mybir.ActivationFunctionType
+ENG = mybir.EngineType
 
 FLOPS = 2 * 512 * 2048 * 4096
 
@@ -21,8 +22,9 @@ KP = 512
 TOK = 512
 GC = 512
 NG = 8
-RAW_BUFS = 10
-V_HALVES = (1, 5, 7)
+RAW_BUFS = 12
+HEAD_SHARE = "VSVSVSVS"
+LOOP_SHARE = "SSSSGGGV"
 
 TWO_PI = 2.0 * math.pi
 C1 = 6.28125
@@ -37,12 +39,14 @@ def tile_attention_pa_kernel(tc, x, Wq, bq, Wk, bk, out_0, out_1):
         xin = ctx.enter_context(tc.tile_pool(name="xin", bufs=4))
         xgp = ctx.enter_context(tc.tile_pool(name="xgp", bufs=4))
         rawp = ctx.enter_context(tc.tile_pool(name="rawp", bufs=RAW_BUFS))
-        grp = ctx.enter_context(tc.tile_pool(name="grp", bufs=4))
+        grp1 = ctx.enter_context(tc.tile_pool(name="grp1", bufs=4))
+        grp2 = ctx.enter_context(tc.tile_pool(name="grp2", bufs=1))
         codes = ctx.enter_context(tc.tile_pool(name="codes", bufs=3))
         up = ctx.enter_context(tc.tile_pool(name="up", bufs=2))
-        op = ctx.enter_context(tc.tile_pool(name="op", bufs=6))
+        op = ctx.enter_context(tc.tile_pool(name="op", bufs=8))
         accp = ctx.enter_context(tc.psum_pool(name="accp", bufs=4))
         trp = ctx.enter_context(tc.psum_pool(name="trp", bufs=4))
+        ctx.enter_context(tc.manual_schedule(engines={ENG.PE, ENG.DVE, ENG.Activation, ENG.Pool}))
 
         zero1 = const.tile([P, 1], F32, name="zero1", tag="zero1")
         nc.vector.memset(zero1[:], 0.0)
@@ -53,14 +57,18 @@ def tile_attention_pa_kernel(tc, x, Wq, bq, Wk, bk, out_0, out_1):
         units = [(G, g) for G in range(NG) for g in range(PASSES)]
         raw_tiles = {}
         x_tiles = {}
+        next_load = [0]
 
         def load_x(g):
             t = xin.tile([P, 4, KP], BF16, name="x_raw", tag="x_raw")
             nc.sync.dma_start(out=t[:], in_=x_view[:, :, g * KP : (g + 1) * KP])
             x_tiles[g] = t
 
-        def load_w(u):
-            G, g = units[u]
+        def load_w():
+            if next_load[0] >= len(units):
+                return
+            G, g = units[next_load[0]]
+            next_load[0] += 1
             w = Wq if G < 4 else Wk
             c0 = (G % 4) * GC
             t = rawp.tile([P, 4, GC], BF16, name="w_raw", tag="w_raw")
@@ -68,7 +76,7 @@ def tile_attention_pa_kernel(tc, x, Wq, bq, Wk, bk, out_0, out_1):
                 out=t[:],
                 in_=w[g * KP : (g + 1) * KP, c0 : c0 + GC].rearrange("(p t) c -> p t c", t=4),
             )
-            raw_tiles[u] = t
+            raw_tiles[(G, g)] = t
 
         bias_rows = const.tile([32, P], BF16, name="bias_rows", tag="bias_rows")
         nc.scalar.dma_start(out=bias_rows[0:16, :], in_=bq.rearrange("(m d) -> m d", d=P))
@@ -76,35 +84,37 @@ def tile_attention_pa_kernel(tc, x, Wq, bq, Wk, bk, out_0, out_1):
 
         for g in range(PASSES):
             load_x(g)
-            load_w(g)
+            load_w()
         for u in range(PASSES, RAW_BUFS):
-            load_w(u)
-        next_load = [RAW_BUFS]
+            load_w()
 
         ident = const.tile([P, P], F32, name="ident", tag="ident")
         make_identity(nc, ident[:])
-        pswap = const.tile([P, P], F32, name="pswap", tag="pswap")
-        ident_v = ident[:].rearrange("p (i e) -> p i e", e=2)
-        pswap_v = pswap[:].rearrange("p (i e) -> p i e", e=2)
-        nc.gpsimd.tensor_copy(out=pswap_v[:, :, 0], in_=ident_v[:, :, 1])
-        nc.gpsimd.tensor_copy(out=pswap_v[:, :, 1], in_=ident_v[:, :, 0])
         pos = const.tile([P, P], F32, name="pos", tag="pos")
         nc.gpsimd.iota(
             pos[:], pattern=[[1, 4], [4, 32]], base=0, channel_multiplier=0,
             allow_small_or_imprecise_dtypes=True,
         )
+        pswap = const.tile([P, P], F32, name="pswap", tag="pswap")
+        ident_v = ident[:].rearrange("p (i e) -> p i e", e=2)
+        pswap_v = pswap[:].rearrange("p (i e) -> p i e", e=2)
+        nc.gpsimd.tensor_copy(out=pswap_v[:, :, 0], in_=ident_v[:, :, 1])
+        nc.gpsimd.tensor_copy(out=pswap_v[:, :, 1], in_=ident_v[:, :, 0])
 
         rows = const.tile([P, 2, P], F32, name="rows", tag="rows")
         nc.vector.memset(rows[:, 0, 0:2], 1.0)
+        sign_v = rows[:, 1, :].rearrange("p (i e) -> p i e", e=2)
+        nc.vector.memset(sign_v[:, :, 0], 1.0)
         for k in range(6):
             w = 2 << k
             nc.vector.tensor_scalar(
                 out=rows[:, 0, w : 2 * w], in0=rows[:, 0, 0:w], scalar1=RATIO ** (1 << k), scalar2=None,
                 op0=ALU.mult,
             )
-        sign_v = rows[:, 1, :].rearrange("p (i e) -> p i e", e=2)
-        nc.vector.memset(sign_v[:, :, 0], 1.0)
-        nc.vector.memset(sign_v[:, :, 1], -1.0)
+            if k == 0:
+                nc.vector.memset(sign_v[:, :, 1], -1.0)
+        bias_sq = const.tile([P, P], F32, name="bias_sq", tag="bias_sq")
+        nc.vector.memset(bias_sq[:], 0.0)
         cols_ps = accp.tile([P, 512], F32, name="cols_ps", tag="acc")
         nc.tensor.transpose(cols_ps[:, 0:P], rows[:, 0, :], ident[:])
         nc.tensor.transpose(cols_ps[:, P : 2 * P], rows[:, 1, :], ident[:])
@@ -113,20 +123,12 @@ def tile_attention_pa_kernel(tc, x, Wq, bq, Wk, bk, out_0, out_1):
         nc.vector.tensor_copy(out=freq[:], in_=cols_ps[:, 0:1])
         nc.vector.tensor_copy(out=sign[:], in_=cols_ps[:, P : P + 1])
 
-        bias_sq = const.tile([P, P], F32, name="bias_sq", tag="bias_sq")
-        nc.vector.memset(bias_sq[:], 0.0)
-        nc.vector.tensor_copy(out=bias_sq[0:32, :], in_=bias_rows[:])
-        bias_ps = accp.tile([P, 512], F32, name="bias_ps", tag="acc")
-        nc.tensor.transpose(bias_ps[:, 0:P], bias_sq[:], ident[:])
-        bias = const.tile([P, 32], F32, name="bias", tag="bias")
-        nc.vector.tensor_copy(out=bias[:], in_=bias_ps[:, 0:32])
-
         ang = const.tile([P, 2, P], F32, name="ang", tag="ang")
         nc.vector.tensor_scalar(
-            out=ang[:, 0, :], in0=pos[:], scalar1=freq[:], scalar2=None, op0=ALU.mult
+            out=ang[:, 0, :], in0=pos[:], scalar1=freq[:], scalar2=0.5 * math.pi, op0=ALU.mult, op1=ALU.add
         )
         nc.vector.tensor_scalar(
-            out=ang[:, 1, :], in0=pos[:], scalar1=freq[:], scalar2=0.5 * math.pi, op0=ALU.mult, op1=ALU.add
+            out=ang[:, 1, :], in0=pos[:], scalar1=freq[:], scalar2=None, op0=ALU.mult
         )
         ang_f = ang[:].rearrange("p a n -> p (a n)")
         turns = const.tile([P, 2 * P], I32, name="turns", tag="turns")
@@ -143,25 +145,35 @@ def tile_attention_pa_kernel(tc, x, Wq, bq, Wk, bk, out_0, out_1):
         )
         over = const.tile([P, 2 * P], F32, name="over", tag="over")
         nc.vector.tensor_scalar(out=over[:], in0=red2[:], scalar1=math.pi, scalar2=None, op0=ALU.is_gt)
-        red3 = const.tile([P, 2, 4, 32], F32, name="red3", tag="red3")
+        red3 = const.tile([P, 2, P], F32, name="red3", tag="red3")
         nc.vector.scalar_tensor_tensor(
-            out=red3[:].rearrange("p a j r -> p (a j r)"), in0=over[:], scalar=-TWO_PI, in1=red2[:],
+            out=red3[:].rearrange("p a n -> p (a n)"), in0=over[:], scalar=-TWO_PI, in1=red2[:],
             op0=ALU.mult, op1=ALU.add,
         )
-        cos_t = const.tile([P, 4, 4, 32], F32, name="cos_t", tag="cos_t")
-        sin_t = const.tile([P, 4, 4, 32], F32, name="sin_t", tag="sin_t")
-        for b in range(4):
-            nc.scalar.activation(out=sin_t[:, :, b, :], in_=red3[:, 0, :, :], func=ACT.Sin, scale=sign[:])
-            nc.scalar.activation(out=cos_t[:, :, b, :], in_=red3[:, 1, :, :], func=ACT.Sin)
-        cos_v = cos_t[:].rearrange("p j b r -> p (j b) r")
-        sin_v = sin_t[:].rearrange("p j b r -> p (j b) r")
+        table = const.tile([P, 2, 4, P], F32, name="table", tag="table")
+
+        def make_table():
+            for b in range(4):
+                nc.scalar.activation(out=table[:, 0, b, :], in_=red3[:, 0, :], func=ACT.Sin)
+                nc.scalar.activation(out=table[:, 1, b, :], in_=red3[:, 1, :], func=ACT.Sin, scale=sign[:])
+
+        bias = const.tile([P, 32], F32, name="bias", tag="bias")
+
+        bias_ps = accp.tile([P, 512], F32, name="bias_ps", tag="acc")
+
+        def turn_bias():
+            nc.vector.tensor_copy(out=bias_sq[0:32, :], in_=bias_rows[:])
+            nc.tensor.transpose(bias_ps[:, 0:P], bias_sq[:], ident[:])
 
         xc = const.tile([P, PASSES, TOK], U32, name="xc", tag="xc", align_bytes=64)
         xs = const.tile([P, PASSES, TOK], U8, name="xs", tag="xs", align_bytes=64)
+        xg_tiles = {}
 
-        def prep_x(g):
+        def turn_x(g):
             xg = xgp.tile([P, TOK, 4], BF16, name="xg", tag="xg", align_bytes=64)
+            xg_tiles[g] = xg
             xg_w = xg[:].rearrange("p c t -> p (c t)").bitcast(F32)
+            xg_v = xg_w.rearrange("p (b j r u) -> p j b r u", b=4, j=4, u=2)
             for jp in range(2):
                 xt = trp.tile([P, 512], F32, name="xt", tag="tr")
                 xt_v = xt[:].rearrange("p (jj u q) -> p jj u q", jj=2, u=2)
@@ -169,100 +181,176 @@ def tile_attention_pa_kernel(tc, x, Wq, bq, Wk, bk, out_0, out_1):
                     words = x_tiles[g][:, 2 * jp + jj, :].bitcast(F32)
                     for u in range(2):
                         nc.tensor.transpose(xt_v[:, jj, u, :], words[:, u:256:2], ident[:])
-                dst = xg_w[:, jp * 512 : (jp + 1) * 512].rearrange("p (jj q u) -> p jj q u", jj=2, u=2)
-                src = xt[:].rearrange("p (jj u q) -> p jj q u", jj=2, u=2)
-                if jp == 0:
-                    nc.vector.tensor_copy(out=dst, in_=src)
-                else:
-                    nc.scalar.copy(out=dst, in_=src)
+                nc.scalar.copy(
+                    out=xg_v[:, 2 * jp : 2 * jp + 2, :, :, :],
+                    in_=xt[:].rearrange("p (jj u b r) -> p jj b r u", jj=2, u=2, b=4),
+                )
+
+        def quantize_x(g):
             nc.vector.quantize_mx(
-                out=xc[:, g, :].bitcast(FP8X4), scales=xs[:, g, :], in_=xg[:].rearrange("p c t -> p (c t)")
+                out=xc[:, g, :].bitcast(FP8X4), scales=xs[:, g, :],
+                in_=xg_tiles.pop(g)[:].rearrange("p c t -> p (c t)"),
             )
 
         w_codes = {}
         grouped = {}
+        copied = {}
 
-        def interleave(u):
-            G, g = units[u]
-            raw = raw_tiles.pop(u)
-            gt = grp.tile([P, GC, 4], BF16, name="w_grouped", tag="w_grouped", align_bytes=64)
-            for half in range(2):
-                cs = slice(half * 256, (half + 1) * 256)
-                src = raw[:, :, cs].rearrange("p t c -> p c t")
-                if 2 * g + half in V_HALVES:
-                    nc.vector.tensor_copy(out=gt[:, cs, :], in_=src)
+        def interleave(G, who):
+            share = HEAD_SHARE if G < 2 else LOOP_SHARE
+            for g in range(PASSES):
+                halves = [hf for hf in range(2) if share[2 * g + hf] == who]
+                if not halves:
+                    continue
+                interleave_unit(G, g, halves, who)
+
+        def interleave_unit(G, g, halves, who):
+            key = (G, g) if g < 2 else (G, 2)
+            if key not in grouped:
+                if g < 2:
+                    grouped[key] = grp1.tile([P, GC, 4], BF16, name="w_g1", tag="w_g1", align_bytes=64)
                 else:
-                    nc.scalar.copy(out=gt[:, cs, :], in_=src)
-            grouped[u] = gt
-            if next_load[0] < len(units):
-                load_w(next_load[0])
-                next_load[0] += 1
+                    grouped[key] = grp2.tile([P, 2 * GC, 4], BF16, name="w_g2", tag="w_g2", align_bytes=64)
+            gt = grouped[key]
+            base = 0 if g < 2 else (g - 2) * GC
+            raw = raw_tiles[(G, g)]
+            lo = halves[0] * 256
+            hi = (halves[-1] + 1) * 256
+            src = raw[:, :, lo:hi].rearrange("p t c -> p c t")
+            dst = gt[:, base + lo : base + hi, :]
+            if who == "V":
+                nc.vector.tensor_copy(out=dst, in_=src)
+            elif who == "S":
+                nc.scalar.copy(out=dst, in_=src)
+            else:
+                nc.gpsimd.tensor_scalar(out=dst, in0=src, scalar1=1.0, scalar2=0.0, op0=ALU.mult, op1=ALU.add)
+            copied[(G, g)] = copied.get((G, g), 0) + len(halves)
+            if copied[(G, g)] == 2:
+                raw_tiles.pop((G, g))
+                load_w()
 
-        def quantize(u):
-            G, g = units[u]
-            if g == 0:
+        def quantize(G, g):
+            if G not in w_codes:
                 wc_new = codes.tile([P, PASSES, GC], U32, name="wc", tag="wc", align_bytes=64)
                 ws_new = codes.tile([P, PASSES, GC], U8, name="ws", tag="ws", align_bytes=64)
                 w_codes[G] = (wc_new, ws_new)
             wc, ws = w_codes[G]
-            gt = grouped.pop(u)
+            n = 1 if g < 2 else 2
+            gt = grouped.pop((G, g))
             nc.vector.quantize_mx(
-                out=wc[:, g, :].bitcast(FP8X4), scales=ws[:, g, :], in_=gt[:].rearrange("p c t -> p (c t)")
+                out=wc[:, g : g + n, :].rearrange("p g c -> p (g c)").bitcast(FP8X4),
+                scales=ws[:, g : g + n, :].rearrange("p g c -> p (g c)"),
+                in_=gt[:].rearrange("p c t -> p (c t)"),
             )
 
-        for g in range(PASSES):
-            prep_x(g)
-            interleave(g)
-            quantize(g)
+        acc_tiles = {}
 
-        for G in range(NG):
-            wc, ws = w_codes.pop(G)
-            u1 = up.tile([P, 16, 4, 32], F32, name="u1", tag="u1")
-            u2 = up.tile([P, 16, 4, 32], F32, name="u2", tag="u2")
-            for h in range(4):
-                hc = slice(h * P, (h + 1) * P)
-                acc = accp.tile([P, 512], F32, name="acc", tag="acc")
-                for g in range(PASSES):
-                    nc.tensor.matmul_mx(
-                        out=acc[:],
-                        lhsT=wc[:, g, hc].bitcast(FP8X4),
-                        lhsT_scale=ws[:, g, hc],
-                        rhs=xc[:, g, :].bitcast(FP8X4),
-                        rhs_scale=xs[:, g, :],
-                        start=(g == 0),
-                        stop=(g == PASSES - 1),
-                    )
-                if G + 1 < NG:
-                    interleave(4 * (G + 1) + h)
-                acc_v = acc[:].rearrange("p (a r) -> p a r", r=32)
-                m = 4 * G + h
+        def project(G, h, passes):
+            wc, ws = w_codes[G]
+            if (G, h) not in acc_tiles:
+                acc_tiles[(G, h)] = accp.tile([P, 512], F32, name="acc", tag="acc")
+            acc = acc_tiles[(G, h)]
+            hc = slice(h * P, (h + 1) * P)
+            for g in passes:
+                nc.tensor.matmul_mx(
+                    out=acc[:],
+                    lhsT=wc[:, g, hc].bitcast(FP8X4),
+                    lhsT_scale=ws[:, g, hc],
+                    rhs=xc[:, g, :].bitcast(FP8X4),
+                    rhs_scale=xs[:, g, :],
+                    start=(g == 0),
+                    stop=(g == PASSES - 1),
+                )
+
+        u_tiles = {}
+
+        def products(G, h, lo, hi):
+            if G not in u_tiles:
+                u_tiles[G] = up.tile([P, 2, 16, 4, 32], F32, name="u", tag="u")
+            u = u_tiles[G]
+            acc = acc_tiles[(G, h)]
+            m = 4 * G + h
+            for tab in range(2):
                 nc.vector.scalar_tensor_tensor(
-                    out=u1[:, :, h, :], in0=acc_v, scalar=bias[:, m : m + 1], in1=cos_v,
+                    out=u[:, tab, 4 * lo : 4 * hi, h, :],
+                    in0=acc[:, P * lo : P * hi].rearrange("p (a r) -> p a r", r=32),
+                    scalar=bias[:, m : m + 1],
+                    in1=table[:, tab, lo:hi, :].rearrange("p b (j r) -> p (b j) r", r=32),
                     op0=ALU.add, op1=ALU.mult,
                 )
-                nc.vector.scalar_tensor_tensor(
-                    out=u2[:, :, h, :], in0=acc_v, scalar=bias[:, m : m + 1], in1=sin_v,
-                    op0=ALU.add, op1=ALU.mult,
-                )
-                if G + 1 < NG:
-                    quantize(4 * (G + 1) + h)
+            if hi == 4:
+                acc_tiles.pop((G, h))
+
+        def rotate_store(G, b):
+            u = u_tiles[G]
             out_m = out_0 if G < 4 else out_1
             scale = 1.0 / math.sqrt(128.0) if G < 4 else 1.0
             h0 = (G % 4) * 4
-            for b in range(4):
-                tr = trp.tile([P, 512], F32, name="tr", tag="tr")
-                for j in range(4):
-                    a = 4 * j + b
-                    nc.tensor.matmul(
-                        out=tr[:, j * P : (j + 1) * P], lhsT=u1[:, a, :, :].rearrange("p h r -> p (h r)"),
-                        rhs=ident[:], start=True, stop=False, is_transpose=True,
-                    )
-                    nc.tensor.matmul(
-                        out=tr[:, j * P : (j + 1) * P], lhsT=u2[:, a, :, :].rearrange("p h r -> p (h r)"),
-                        rhs=pswap[:], start=False, stop=True, is_transpose=True,
-                    )
-                o = op.tile([P, 512], F32, name="o", tag="o")
-                nc.scalar.activation(out=o[:], in_=tr[:], func=ACT.Copy, scale=scale)
-                nc.sync.dma_start(
-                    out=out_m[b, h0 : h0 + 4, :, :].rearrange("h (r j) d -> (h r) (j d)", j=4), in_=o[:]
+            tr = trp.tile([P, 512], F32, name="tr", tag="tr")
+            for j in range(4):
+                a = 4 * b + j
+                nc.tensor.matmul(
+                    out=tr[:, j * P : (j + 1) * P], lhsT=u[:, 0, a, :, :].rearrange("p h r -> p (h r)"),
+                    rhs=ident[:], start=True, stop=False, is_transpose=True,
                 )
+                nc.tensor.matmul(
+                    out=tr[:, j * P : (j + 1) * P], lhsT=u[:, 1, a, :, :].rearrange("p h r -> p (h r)"),
+                    rhs=pswap[:], start=False, stop=True, is_transpose=True,
+                )
+            o = op.tile([P, 512], F32, name="o", tag="o")
+            nc.scalar.activation(out=o[:], in_=tr[:], func=ACT.Copy, scale=scale)
+            nc.sync.dma_start(
+                out=out_m[b, h0 : h0 + 4, :, :].rearrange("h (r j) d -> (h r) (j d)", j=4), in_=o[:]
+            )
+
+        for g in range(PASSES):
+            turn_x(g)
+            if g == 0:
+                turn_bias()
+            for hf in range(2):
+                interleave_unit(0, g, [hf], HEAD_SHARE[2 * g + hf])
+            quantize_x(g)
+            if g == 0:
+                nc.vector.tensor_copy(out=bias[:], in_=bias_ps[:, 0:32])
+            if g == 1:
+                make_table()
+            if g < 2:
+                quantize(0, g)
+            if g >= 1 and g - 1 < 2:
+                for h in range(4):
+                    project(0, h, [g - 1])
+        quantize(0, 2)
+        for h in range(4):
+            project(0, h, [2, 3])
+
+        for g in range(PASSES):
+            for hf in range(2):
+                interleave_unit(1, g, [hf], HEAD_SHARE[2 * g + hf])
+            if 1 <= g <= 2:
+                quantize(1, g - 1)
+        quantize(1, 2)
+
+        for c in range(NG):
+            if c + 2 < NG:
+                interleave(c + 2, "G")
+            s_units = [g for g in range(PASSES) if "S" in LOOP_SHARE[2 * g : 2 * g + 2]]
+            if c < NG - 1:
+                for h in range(4):
+                    products(c, h, 0, 4)
+                    project(c + 1, h, range(PASSES))
+                    if c + 2 < NG and h < len(s_units):
+                        g = s_units[h]
+                        interleave_unit(c + 2, g, [hf for hf in range(2) if LOOP_SHARE[2 * g + hf] == "S"], "S")
+                for b in range(4):
+                    rotate_store(c, b)
+            else:
+                for half in range(2):
+                    for h in range(4):
+                        products(c, h, 2 * half, 2 * half + 2)
+                    for b in range(2 * half, 2 * half + 2):
+                        rotate_store(c, b)
+            if c + 2 < NG:
+                interleave(c + 2, "V")
+                quantize(c + 2, 0)
+                quantize(c + 2, 1)
+                quantize(c + 2, 2)

@@ -218,10 +218,12 @@ def tile_attention_pa_kernel(tc, x, Wq, bq, Wk, bk, out_0, out_1):
             hi = (halves[-1] + 1) * 256
             src = raw[:, :, lo:hi].rearrange("p t c -> p c t")
             dst = gt[:, base + lo : base + hi, :]
+            src4 = raw[:, :, lo:hi].rearrange("p t (c i) -> p c t i", i=4)
+            dst4 = dst.rearrange("p (c i) t -> p c t i", i=4)
             if who == "V":
-                nc.vector.tensor_copy(out=dst, in_=src)
+                nc.vector.tensor_copy(out=dst4, in_=src4)
             elif who == "S":
-                nc.scalar.copy(out=dst, in_=src)
+                nc.scalar.copy(out=dst4, in_=src4)
             else:
                 nc.gpsimd.tensor_scalar(out=dst, in0=src, scalar1=1.0, scalar2=0.0, op0=ALU.mult, op1=ALU.add)
             copied[(G, g)] = copied.get((G, g), 0) + len(halves)
@@ -270,14 +272,23 @@ def tile_attention_pa_kernel(tc, x, Wq, bq, Wk, bk, out_0, out_1):
             u = u_tiles[G]
             acc = acc_tiles[(G, h)]
             m = 4 * G + h
-            for tab in range(2):
+            if lo == 0 and hi == 4:
                 nc.vector.scalar_tensor_tensor(
-                    out=u[:, tab, 4 * lo : 4 * hi, h, :],
-                    in0=acc[:, P * lo : P * hi].rearrange("p (a r) -> p a r", r=32),
+                    out=u[:, :, :, h, :],
+                    in0=acc[:].rearrange("p (o a r) -> p o a r", o=1, r=32).to_broadcast([P, 2, 16, 32]),
                     scalar=bias[:, m : m + 1],
-                    in1=table[:, tab, lo:hi, :].rearrange("p b (j r) -> p (b j) r", r=32),
+                    in1=table[:].rearrange("p t b (j r) -> p t (b j) r", r=32),
                     op0=ALU.add, op1=ALU.mult,
                 )
+            else:
+                for tab in range(2):
+                    nc.vector.scalar_tensor_tensor(
+                        out=u[:, tab, 4 * lo : 4 * hi, h, :],
+                        in0=acc[:, P * lo : P * hi].rearrange("p (a r) -> p a r", r=32),
+                        scalar=bias[:, m : m + 1],
+                        in1=table[:, tab, lo:hi, :].rearrange("p b (j r) -> p (b j) r", r=32),
+                        op0=ALU.add, op1=ALU.mult,
+                    )
             if hi == 4:
                 acc_tiles.pop((G, h))
 

@@ -23,8 +23,9 @@ TOK = 512
 GC = 512
 NG = 8
 RAW_BUFS = 12
-HEAD_SHARE = "VSVSVSVS"
+HEAD_SHARE = ("VVVSVSVS", "VSVSVSVS")
 LOOP_SHARE = "SSSSGGGV"
+S_LEAD = 6
 
 TWO_PI = 2.0 * math.pi
 C1 = 6.28125
@@ -39,7 +40,7 @@ def tile_attention_pa_kernel(tc, x, Wq, bq, Wk, bk, out_0, out_1):
         xin = ctx.enter_context(tc.tile_pool(name="xin", bufs=4))
         xgp = ctx.enter_context(tc.tile_pool(name="xgp", bufs=4))
         rawp = ctx.enter_context(tc.tile_pool(name="rawp", bufs=RAW_BUFS))
-        grp1 = ctx.enter_context(tc.tile_pool(name="grp1", bufs=4))
+        grp1 = ctx.enter_context(tc.tile_pool(name="grp1", bufs=6))
         grp2 = ctx.enter_context(tc.tile_pool(name="grp2", bufs=1))
         codes = ctx.enter_context(tc.tile_pool(name="codes", bufs=3))
         up = ctx.enter_context(tc.tile_pool(name="up", bufs=2))
@@ -153,9 +154,12 @@ def tile_attention_pa_kernel(tc, x, Wq, bq, Wk, bk, out_0, out_1):
         table = const.tile([P, 2, 4, P], F32, name="table", tag="table")
 
         def make_table():
-            for b in range(4):
-                nc.scalar.activation(out=table[:, 0, b, :], in_=red3[:, 0, :], func=ACT.Sin)
-                nc.scalar.activation(out=table[:, 1, b, :], in_=red3[:, 1, :], func=ACT.Sin, scale=sign[:])
+            nc.scalar.activation(out=table[:, 0, 0, :], in_=red3[:, 0, :], func=ACT.Sin)
+            nc.scalar.activation(out=table[:, 1, 0, :], in_=red3[:, 1, :], func=ACT.Sin, scale=sign[:])
+            for b in range(1, 4):
+                nc.gpsimd.tensor_scalar(
+                    out=table[:, :, b, :], in0=table[:, :, 0, :], scalar1=1.0, scalar2=0.0, op0=ALU.mult, op1=ALU.add
+                )
 
         bias = const.tile([P, 32], F32, name="bias", tag="bias")
 
@@ -197,7 +201,7 @@ def tile_attention_pa_kernel(tc, x, Wq, bq, Wk, bk, out_0, out_1):
         copied = {}
 
         def interleave(G, who):
-            share = HEAD_SHARE if G < 2 else LOOP_SHARE
+            share = HEAD_SHARE[G] if G < 2 else LOOP_SHARE
             for g in range(PASSES):
                 halves = [hf for hf in range(2) if share[2 * g + hf] == who]
                 if not halves:
@@ -319,7 +323,7 @@ def tile_attention_pa_kernel(tc, x, Wq, bq, Wk, bk, out_0, out_1):
             if g == 0:
                 turn_bias()
             for hf in range(2):
-                interleave_unit(0, g, [hf], HEAD_SHARE[2 * g + hf])
+                interleave_unit(0, g, [hf], HEAD_SHARE[0][2 * g + hf])
             quantize_x(g)
             if g == 0:
                 nc.vector.tensor_copy(out=bias[:], in_=bias_ps[:, 0:32])
@@ -336,24 +340,32 @@ def tile_attention_pa_kernel(tc, x, Wq, bq, Wk, bk, out_0, out_1):
 
         for g in range(PASSES):
             for hf in range(2):
-                interleave_unit(1, g, [hf], HEAD_SHARE[2 * g + hf])
+                interleave_unit(1, g, [hf], HEAD_SHARE[1][2 * g + hf])
             if 1 <= g <= 2:
                 quantize(1, g - 1)
         quantize(1, 2)
 
+        s_stream = [
+            (G, g, hf) for G in range(2, NG) for g in range(PASSES) for hf in range(2) if LOOP_SHARE[2 * g + hf] == "S"
+        ]
+
+        def scalar_next():
+            if s_stream:
+                G, g, hf = s_stream.pop(0)
+                interleave_unit(G, g, [hf], "S")
+
+        for i in range(S_LEAD):
+            scalar_next()
         for c in range(NG):
             if c + 2 < NG:
                 interleave(c + 2, "G")
-            s_units = [g for g in range(PASSES) if "S" in LOOP_SHARE[2 * g : 2 * g + 2]]
             if c < NG - 1:
                 for h in range(4):
                     products(c, h, 0, 4)
                     project(c + 1, h, range(PASSES))
-                    if c + 2 < NG and h < len(s_units):
-                        g = s_units[h]
-                        interleave_unit(c + 2, g, [hf for hf in range(2) if LOOP_SHARE[2 * g + hf] == "S"], "S")
                 for b in range(4):
                     rotate_store(c, b)
+                    scalar_next()
             else:
                 for half in range(2):
                     for h in range(4):

@@ -25,6 +25,7 @@ NG = 8
 RAW_BUFS = 12
 HEAD_SHARE = ("VVVSVSVS", "VSVSVSVS")
 LOOP_SHARE = "SSSSGGGV"
+GROUP2_SHARE = "SSSSGGSV"
 S_LEAD = 6
 
 TWO_PI = 2.0 * math.pi
@@ -200,8 +201,13 @@ def tile_attention_pa_kernel(tc, x, Wq, bq, Wk, bk, out_0, out_1):
         grouped = {}
         copied = {}
 
+        def share_of(G):
+            if G < 2:
+                return HEAD_SHARE[G]
+            return GROUP2_SHARE if G == 2 else LOOP_SHARE
+
         def interleave(G, who):
-            share = HEAD_SHARE[G] if G < 2 else LOOP_SHARE
+            share = share_of(G)
             for g in range(PASSES):
                 halves = [hf for hf in range(2) if share[2 * g + hf] == who]
                 if not halves:
@@ -235,18 +241,24 @@ def tile_attention_pa_kernel(tc, x, Wq, bq, Wk, bk, out_0, out_1):
                 raw_tiles.pop((G, g))
                 load_w()
 
-        def quantize(G, g):
+        def quantize(G, g, n):
             if G not in w_codes:
                 wc_new = codes.tile([P, PASSES, GC], U32, name="wc", tag="wc", align_bytes=64)
                 ws_new = codes.tile([P, PASSES, GC], U8, name="ws", tag="ws", align_bytes=64)
                 w_codes[G] = (wc_new, ws_new)
             wc, ws = w_codes[G]
-            n = 1 if g < 2 else 2
-            gt = grouped.pop((G, g))
+            if g < 2:
+                gt = grouped.pop((G, g))
+                base = 0
+            else:
+                gt = grouped[(G, 2)]
+                base = (g - 2) * GC
+                if g + n == PASSES:
+                    grouped.pop((G, 2))
             nc.vector.quantize_mx(
                 out=wc[:, g : g + n, :].rearrange("p g c -> p (g c)").bitcast(FP8X4),
                 scales=ws[:, g : g + n, :].rearrange("p g c -> p (g c)"),
-                in_=gt[:].rearrange("p c t -> p (c t)"),
+                in_=gt[:, base : base + n * GC, :].rearrange("p c t -> p (c t)"),
             )
 
         acc_tiles = {}
@@ -330,23 +342,25 @@ def tile_attention_pa_kernel(tc, x, Wq, bq, Wk, bk, out_0, out_1):
             if g == 1:
                 make_table()
             if g < 2:
-                quantize(0, g)
+                quantize(0, g, 1)
             if g >= 1 and g - 1 < 2:
                 for h in range(4):
                     project(0, h, [g - 1])
-        quantize(0, 2)
+        quantize(0, 2, 2)
         for h in range(4):
             project(0, h, [2, 3])
 
         for g in range(PASSES):
             for hf in range(2):
                 interleave_unit(1, g, [hf], HEAD_SHARE[1][2 * g + hf])
-            if 1 <= g <= 2:
-                quantize(1, g - 1)
-        quantize(1, 2)
+            if g >= 1:
+                quantize(1, g - 1, 1)
+            if g == 2:
+                products(0, 0, 0, 4)
+        quantize(1, 3, 1)
 
         s_stream = [
-            (G, g, hf) for G in range(2, NG) for g in range(PASSES) for hf in range(2) if LOOP_SHARE[2 * g + hf] == "S"
+            (G, g, hf) for G in range(2, NG) for g in range(PASSES) for hf in range(2) if share_of(G)[2 * g + hf] == "S"
         ]
 
         def scalar_next():
@@ -361,7 +375,8 @@ def tile_attention_pa_kernel(tc, x, Wq, bq, Wk, bk, out_0, out_1):
                 interleave(c + 2, "G")
             if c < NG - 1:
                 for h in range(4):
-                    products(c, h, 0, 4)
+                    if c > 0 or h > 0:
+                        products(c, h, 0, 4)
                     project(c + 1, h, range(PASSES))
                 for b in range(4):
                     rotate_store(c, b)
@@ -374,6 +389,6 @@ def tile_attention_pa_kernel(tc, x, Wq, bq, Wk, bk, out_0, out_1):
                         rotate_store(c, b)
             if c + 2 < NG:
                 interleave(c + 2, "V")
-                quantize(c + 2, 0)
-                quantize(c + 2, 1)
-                quantize(c + 2, 2)
+                quantize(c + 2, 0, 1)
+                quantize(c + 2, 1, 1)
+                quantize(c + 2, 2, 2)

@@ -50,6 +50,10 @@ def tile_attention_pa_kernel(tc, x, Wq, bq, Wk, bk, out_0, out_1):
         trp = ctx.enter_context(tc.psum_pool(name="trp", bufs=4))
         ctx.enter_context(tc.manual_schedule(engines={ENG.PE, ENG.DVE, ENG.Activation, ENG.Pool}))
 
+        bias_rows = const.tile([32, P], BF16, name="bias_rows", tag="bias_rows")
+        nc.scalar.dma_start(out=bias_rows[0:16, :], in_=bq.rearrange("(m d) -> m d", d=P))
+        nc.scalar.dma_start(out=bias_rows[16:32, :], in_=bk.rearrange("(m d) -> m d", d=P))
+
         zero1 = const.tile([P, 1], F32, name="zero1", tag="zero1")
         nc.vector.memset(zero1[:], 0.0)
         warm = const.tile([P, 1], F32, name="warm", tag="warm")
@@ -79,10 +83,6 @@ def tile_attention_pa_kernel(tc, x, Wq, bq, Wk, bk, out_0, out_1):
                 in_=w[g * KP : (g + 1) * KP, c0 : c0 + GC].rearrange("(p t) c -> p t c", t=4),
             )
             raw_tiles[(G, g)] = t
-
-        bias_rows = const.tile([32, P], BF16, name="bias_rows", tag="bias_rows")
-        nc.scalar.dma_start(out=bias_rows[0:16, :], in_=bq.rearrange("(m d) -> m d", d=P))
-        nc.scalar.dma_start(out=bias_rows[16:32, :], in_=bk.rearrange("(m d) -> m d", d=P))
 
         for g in range(PASSES):
             load_x(g)
@@ -332,23 +332,21 @@ def tile_attention_pa_kernel(tc, x, Wq, bq, Wk, bk, out_0, out_1):
 
         for g in range(PASSES):
             turn_x(g)
-            if g == 0:
+            if g == 1:
                 turn_bias()
             for hf in range(2):
                 interleave_unit(0, g, [hf], HEAD_SHARE[0][2 * g + hf])
             quantize_x(g)
-            if g == 0:
+            if g == 1:
                 nc.vector.tensor_copy(out=bias[:], in_=bias_ps[:, 0:32])
             if g == 1:
                 make_table()
-            if g < 2:
-                quantize(0, g, 1)
-            if g >= 1 and g - 1 < 2:
+            quantize(0, g, 1)
+            if g >= 1:
                 for h in range(4):
                     project(0, h, [g - 1])
-        quantize(0, 2, 2)
         for h in range(4):
-            project(0, h, [2, 3])
+            project(0, h, [3])
 
         for g in range(PASSES):
             for hf in range(2):

@@ -86,8 +86,7 @@ def tile_attention_pa_kernel(tc, x, Wq, bq, Wk, bk, out_0, out_1):
 
         for g in range(PASSES):
             load_x(g)
-            load_w()
-        for u in range(PASSES, RAW_BUFS):
+        for u in range(RAW_BUFS):
             load_w()
 
         ident = const.tile([P, P], F32, name="ident", tag="ident")
@@ -155,11 +154,10 @@ def tile_attention_pa_kernel(tc, x, Wq, bq, Wk, bk, out_0, out_1):
         table = const.tile([P, 2, 4, P], F32, name="table", tag="table")
 
         def make_table():
-            nc.scalar.activation(out=table[:, 0, 0, :], in_=red3[:, 0, :], func=ACT.Sin)
-            nc.scalar.activation(out=table[:, 1, 0, :], in_=red3[:, 1, :], func=ACT.Sin, scale=sign[:])
-            for b in range(1, 4):
-                nc.gpsimd.tensor_scalar(
-                    out=table[:, :, b, :], in0=table[:, :, 0, :], scalar1=1.0, scalar2=0.0, op0=ALU.mult, op1=ALU.add
+            for tab in range(2):
+                nc.scalar.activation(
+                    out=table[:, tab, :, :], in_=red3[:, tab : tab + 1, :].to_broadcast([P, 4, P]), func=ACT.Sin,
+                    scale=(sign[:] if tab == 1 else 1.0),
                 )
 
         bias = const.tile([P, 32], F32, name="bias", tag="bias")
@@ -266,7 +264,10 @@ def tile_attention_pa_kernel(tc, x, Wq, bq, Wk, bk, out_0, out_1):
         def project(G, h, passes):
             wc, ws = w_codes[G]
             if (G, h) not in acc_tiles:
-                acc_tiles[(G, h)] = accp.tile([P, 512], F32, name="acc", tag="acc")
+                if G == 0:
+                    acc_tiles[(G, h)] = accp.tile([P, 512], F32, name="acc", tag="acc")
+                else:
+                    acc_tiles[(G, h)] = trp.tile([P, 512], F32, name="acc1", tag="tr")
             acc = acc_tiles[(G, h)]
             hc = slice(h * P, (h + 1) * P)
             for g in passes:
@@ -313,7 +314,7 @@ def tile_attention_pa_kernel(tc, x, Wq, bq, Wk, bk, out_0, out_1):
             out_m = out_0 if G < 4 else out_1
             scale = 1.0 / math.sqrt(128.0) if G < 4 else 1.0
             h0 = (G % 4) * 4
-            tr = trp.tile([P, 512], F32, name="tr", tag="tr")
+            tr = accp.tile([P, 512], F32, name="tr", tag="acc")
             for j in range(4):
                 a = 4 * b + j
                 nc.tensor.matmul(
@@ -334,17 +335,21 @@ def tile_attention_pa_kernel(tc, x, Wq, bq, Wk, bk, out_0, out_1):
             turn_x(g)
             if g == 1:
                 turn_bias()
+            if g >= 1:
+                quantize_x(g - 1)
+            if g == 2:
+                nc.vector.tensor_copy(out=bias[:], in_=bias_ps[:, 0:32])
+        make_table()
+        for g in range(PASSES):
             for hf in range(2):
                 interleave_unit(0, g, [hf], HEAD_SHARE[0][2 * g + hf])
-            quantize_x(g)
-            if g == 1:
-                nc.vector.tensor_copy(out=bias[:], in_=bias_ps[:, 0:32])
-            if g == 1:
-                make_table()
-            quantize(0, g, 1)
+            if g == 0:
+                quantize_x(3)
             if g >= 1:
+                quantize(0, g - 1, 1)
                 for h in range(4):
                     project(0, h, [g - 1])
+        quantize(0, 3, 1)
         for h in range(4):
             project(0, h, [3])
 
@@ -353,9 +358,13 @@ def tile_attention_pa_kernel(tc, x, Wq, bq, Wk, bk, out_0, out_1):
                 interleave_unit(1, g, [hf], HEAD_SHARE[1][2 * g + hf])
             if g >= 1:
                 quantize(1, g - 1, 1)
+                for h in range(4):
+                    project(1, h, [g - 1])
             if g == 2:
                 products(0, 0, 0, 4)
         quantize(1, 3, 1)
+        for h in range(4):
+            project(1, h, [3])
 
         s_stream = [
             (G, g, hf) for G in range(2, NG) for g in range(PASSES) for hf in range(2) if share_of(G)[2 * g + hf] == "S"
@@ -375,7 +384,8 @@ def tile_attention_pa_kernel(tc, x, Wq, bq, Wk, bk, out_0, out_1):
                 for h in range(4):
                     if c > 0 or h > 0:
                         products(c, h, 0, 4)
-                    project(c + 1, h, range(PASSES))
+                    if c > 0:
+                        project(c + 1, h, range(PASSES))
                 for b in range(4):
                     rotate_store(c, b)
                     scalar_next()

import math
from contextlib import ExitStack

import concourse.mybir as mybir
from concourse.masks import make_identity

F32 = mybir.dt.float32
BF16 = mybir.dt.bfloat16
U32 = mybir.dt.uint32
U8 = mybir.dt.uint8
I32 = mybir.dt.int32
FP8X4 = mybir.dt.float8_e5m2_x4
ALU = mybir.AluOpType
ACT = mybir.ActivationFunctionType
ENG = mybir.EngineType

FLOPS = 2 * 512 * 2048 * 4096

P = 128
PASSES = 4
KP = 512
TOK = 512
GC = 512
NG = 8
RAW_BUFS = 12
HEAD_SHARE = ("VVVSVSVS", "VSVSVSVS")
LOOP_SHARE = "SSSSGGGV"
GROUP2_SHARE = "SSSSGGSV"
S_LEAD = 6

TWO_PI = 2.0 * math.pi
C1 = 6.28125
C2 = TWO_PI - C1
RATIO = 10000.0 ** (-1.0 / 64.0)


def tile_attention_pa_kernel(tc, x, Wq, bq, Wk, bk, out_0, out_1):
    nc = tc.nc
    with ExitStack() as ctx:
        const = ctx.enter_context(tc.tile_pool(name="const", bufs=1))
        xin = ctx.enter_context(tc.tile_pool(name="xin", bufs=4))
        xgp = ctx.enter_context(tc.tile_pool(name="xgp", bufs=4))
        rawp = ctx.enter_context(tc.tile_pool(name="rawp", bufs=RAW_BUFS))
        grp1 = ctx.enter_context(tc.tile_pool(name="grp1", bufs=6))
        grp2 = ctx.enter_context(tc.tile_pool(name="grp2", bufs=1))
        codes = ctx.enter_context(tc.tile_pool(name="codes", bufs=3))
        up = ctx.enter_context(tc.tile_pool(name="up", bufs=2))
        op = ctx.enter_context(tc.tile_pool(name="op", bufs=8))
        accp = ctx.enter_context(tc.psum_pool(name="accp", bufs=4))
        trp = ctx.enter_context(tc.psum_pool(name="trp", bufs=4))
        ctx.enter_context(tc.manual_schedule(engines={ENG.PE, ENG.DVE, ENG.Activation, ENG.Pool}))

        bias_rows = const.tile([32, P], BF16, name="bias_rows", tag="bias_rows")
        nc.scalar.dma_start(out=bias_rows[0:16, :], in_=bq.rearrange("(m d) -> m d", d=P))
        nc.scalar.dma_start(out=bias_rows[16:32, :], in_=bk.rearrange("(m d) -> m d", d=P))

        zero1 = const.tile([P, 1], F32, name="zero1", tag="zero1")
        nc.vector.memset(zero1[:], 0.0)
        warm = const.tile([P, 1], F32, name="warm", tag="warm")
        nc.scalar.activation(out=warm[:], in_=zero1[:], func=ACT.Sin)

        x_view = x.flatten_outer_dims().rearrange("(q j) k -> q j k", j=4)
        units = [(G, g) for G in range(NG) for g in range(PASSES)]
        raw_tiles = {}
        x_tiles = {}
        next_load = [0]

        def load_x(g):
            t = xin.tile([P, 4, KP], BF16, name="x_raw", tag="x_raw")
            nc.sync.dma_start(out=t[:], in_=x_view[:, :, g * KP : (g + 1) * KP])
            x_tiles[g] = t

        def load_w():
            if next_load[0] >= len(units):
                return
            G, g = units[next_load[0]]
            next_load[0] += 1
            w = Wq if G < 4 else Wk
            c0 = (G % 4) * GC
            t = rawp.tile([P, 4, GC], BF16, name="w_raw", tag="w_raw")
            nc.sync.dma_start(
                out=t[:],
                in_=w[g * KP : (g + 1) * KP, c0 : c0 + GC].rearrange("(p t) c -> p t c", t=4),
            )
            raw_tiles[(G, g)] = t

        for g in range(PASSES):
            load_x(g)
        for u in range(RAW_BUFS):
            load_w()

        ident = const.tile([P, P], F32, name="ident", tag="ident")
        make_identity(nc, ident[:])
        pos = const.tile([P, P], F32, name="pos", tag="pos")
        nc.gpsimd.iota(
            pos[:], pattern=[[1, 4], [4, 32]], base=0, channel_multiplier=0,
            allow_small_or_imprecise_dtypes=True,
        )
        pswap = const.tile([P, P], F32, name="pswap", tag="pswap")
        ident_v = ident[:].rearrange("p (i e) -> p i e", e=2)
        pswap_v = pswap[:].rearrange("p (i e) -> p i e", e=2)
        nc.gpsimd.tensor_copy(out=pswap_v[:, :, 0], in_=ident_v[:, :, 1])
        nc.gpsimd.tensor_copy(out=pswap_v[:, :, 1], in_=ident_v[:, :, 0])

        rows = const.tile([P, 2, P], F32, name="rows", tag="rows")
        nc.vector.memset(rows[:, 0, 0:2], 1.0)
        sign_v = rows[:, 1, :].rearrange("p (i e) -> p i e", e=2)
        nc.vector.memset(sign_v[:, :, 0], 1.0)
        for k in range(6):
            w = 2 << k
            nc.vector.tensor_scalar(
                out=rows[:, 0, w : 2 * w], in0=rows[:, 0, 0:w], scalar1=RATIO ** (1 << k), scalar2=None,
                op0=ALU.mult,
            )
            if k == 0:
                nc.vector.memset(sign_v[:, :, 1], -1.0)
        bias_sq = const.tile([P, P], F32, name="bias_sq", tag="bias_sq")
        nc.vector.memset(bias_sq[:], 0.0)
        cols_ps = accp.tile([P, 512], F32, name="cols_ps", tag="acc")
        nc.tensor.transpose(cols_ps[:, 0:P], rows[:, 0, :], ident[:])
        nc.tensor.transpose(cols_ps[:, P : 2 * P], rows[:, 1, :], ident[:])
        freq = const.tile([P, 1], F32, name="freq", tag="freq")
        sign = const.tile([P, 1], F32, name="sign", tag="sign")
        nc.vector.tensor_copy(out=freq[:], in_=cols_ps[:, 0:1])
        nc.vector.tensor_copy(out=sign[:], in_=cols_ps[:, P : P + 1])

        ang = const.tile([P, 2, P], F32, name="ang", tag="ang")
        nc.vector.tensor_scalar(
            out=ang[:, 0, :], in0=pos[:], scalar1=freq[:], scalar2=0.5 * math.pi, op0=ALU.mult, op1=ALU.add
        )
        nc.vector.tensor_scalar(
            out=ang[:, 1, :], in0=pos[:], scalar1=freq[:], scalar2=None, op0=ALU.mult
        )
        ang_f = ang[:].rearrange("p a n -> p (a n)")
        turns = const.tile([P, 2 * P], I32, name="turns", tag="turns")
        nc.vector.tensor_scalar(
            out=turns[:], in0=ang_f, scalar1=1.0 / TWO_PI, scalar2=None, op0=ALU.mult
        )
        red1 = const.tile([P, 2 * P], F32, name="red1", tag="red1")
        nc.vector.scalar_tensor_tensor(
            out=red1[:], in0=turns[:], scalar=-C1, in1=ang_f, op0=ALU.mult, op1=ALU.add
        )
        red2 = const.tile([P, 2 * P], F32, name="red2", tag="red2")
        nc.vector.scalar_tensor_tensor(
            out=red2[:], in0=turns[:], scalar=-C2, in1=red1[:], op0=ALU.mult, op1=ALU.add
        )
        over = const.tile([P, 2 * P], F32, name="over", tag="over")
        nc.vector.tensor_scalar(out=over[:], in0=red2[:], scalar1=math.pi, scalar2=None, op0=ALU.is_gt)
        red3 = const.tile([P, 2, P], F32, name="red3", tag="red3")
        nc.vector.scalar_tensor_tensor(
            out=red3[:].rearrange("p a n -> p (a n)"), in0=over[:], scalar=-TWO_PI, in1=red2[:],
            op0=ALU.mult, op1=ALU.add,
        )
        table = const.tile([P, 2, 4, P], F32, name="table", tag="table")

        def make_table():
            for tab in range(2):
                nc.scalar.activation(
                    out=table[:, tab, :, :], in_=red3[:, tab : tab + 1, :].to_broadcast([P, 4, P]), func=ACT.Sin,
                    scale=(sign[:] if tab == 1 else 1.0),
                )

        bias = const.tile([P, 32], F32, name="bias", tag="bias")

        bias_ps = accp.tile([P, 512], F32, name="bias_ps", tag="acc")

        def turn_bias():
            nc.vector.tensor_copy(out=bias_sq[0:32, :], in_=bias_rows[:])
            nc.tensor.transpose(bias_ps[:, 0:P], bias_sq[:], ident[:])

        xc = const.tile([P, PASSES, TOK], U32, name="xc", tag="xc", align_bytes=64)
        xs = const.tile([P, PASSES, TOK], U8, name="xs", tag="xs", align_bytes=64)
        xg_tiles = {}

        def turn_x(g):
            xg = xgp.tile([P, TOK, 4], BF16, name="xg", tag="xg", align_bytes=64)
            xg_tiles[g] = xg
            xg_w = xg[:].rearrange("p c t -> p (c t)").bitcast(F32)
            xg_v = xg_w.rearrange("p (b j r u) -> p j b r u", b=4, j=4, u=2)
            for jp in range(2):
                xt = trp.tile([P, 512], F32, name="xt", tag="tr")
                xt_v = xt[:].rearrange("p (jj u q) -> p jj u q", jj=2, u=2)
                for jj in range(2):
                    words = x_tiles[g][:, 2 * jp + jj, :].bitcast(F32)
                    for u in range(2):
                        nc.tensor.transpose(xt_v[:, jj, u, :], words[:, u:256:2], ident[:])
                nc.scalar.copy(
                    out=xg_v[:, 2 * jp : 2 * jp + 2, :, :, :],
                    in_=xt[:].rearrange("p (jj u b r) -> p jj b r u", jj=2, u=2, b=4),
                )

        def quantize_x(g):
            nc.vector.quantize_mx(
                out=xc[:, g, :].bitcast(FP8X4), scales=xs[:, g, :],
                in_=xg_tiles.pop(g)[:].rearrange("p c t -> p (c t)"),
            )

        w_codes = {}
        grouped = {}
        copied = {}

        def share_of(G):
            if G < 2:
                return HEAD_SHARE[G]
            return GROUP2_SHARE if G == 2 else LOOP_SHARE

        def interleave(G, who):
            share = share_of(G)
            for g in range(PASSES):
                halves = [hf for hf in range(2) if share[2 * g + hf] == who]
                if not halves:
                    continue
                interleave_unit(G, g, halves, who)

        def interleave_unit(G, g, halves, who):
            key = (G, g) if g < 2 else (G, 2)
            if key not in grouped:
                if g < 2:
                    grouped[key] = grp1.tile([P, GC, 4], BF16, name="w_g1", tag="w_g1", align_bytes=64)
                else:
                    grouped[key] = grp2.tile([P, 2 * GC, 4], BF16, name="w_g2", tag="w_g2", align_bytes=64)
            gt = grouped[key]
            base = 0 if g < 2 else (g - 2) * GC
            raw = raw_tiles[(G, g)]
            lo = halves[0] * 256
            hi = (halves[-1] + 1) * 256
            src = raw[:, :, lo:hi].rearrange("p t c -> p c t")
            dst = gt[:, base + lo : base + hi, :]
            src4 = raw[:, :, lo:hi].rearrange("p t (c i) -> p c t i", i=4)
            dst4 = dst.rearrange("p (c i) t -> p c t i", i=4)
            if who == "V":
                nc.vector.tensor_copy(out=dst4, in_=src4)
            elif who == "S":
                nc.scalar.copy(out=dst4, in_=src4)
            else:
                nc.gpsimd.tensor_scalar(out=dst, in0=src, scalar1=1.0, scalar2=0.0, op0=ALU.mult, op1=ALU.add)
            copied[(G, g)] = copied.get((G, g), 0) + len(halves)
            if copied[(G, g)] == 2:
                raw_tiles.pop((G, g))
                load_w()

        def quantize(G, g, n):
            if G not in w_codes:
                wc_new = codes.tile([P, PASSES, GC], U32, name="wc", tag="wc", align_bytes=64)
                ws_new = codes.tile([P, PASSES, GC], U8, name="ws", tag="ws", align_bytes=64)
                w_codes[G] = (wc_new, ws_new)
            wc, ws = w_codes[G]
            if g < 2:
                gt = grouped.pop((G, g))
                base = 0
            else:
                gt = grouped[(G, 2)]
                base = (g - 2) * GC
                if g + n == PASSES:
                    grouped.pop((G, 2))
            nc.vector.quantize_mx(
                out=wc[:, g : g + n, :].rearrange("p g c -> p (g c)").bitcast(FP8X4),
                scales=ws[:, g : g + n, :].rearrange("p g c -> p (g c)"),
                in_=gt[:, base : base + n * GC, :].rearrange("p c t -> p (c t)"),
            )

        acc_tiles = {}

        def project(G, h, passes):
            wc, ws = w_codes[G]
            if (G, h) not in acc_tiles:
                if G == 0:
                    acc_tiles[(G, h)] = accp.tile([P, 512], F32, name="acc", tag="acc")
                else:
                    acc_tiles[(G, h)] = trp.tile([P, 512], F32, name="acc1", tag="tr")
            acc = acc_tiles[(G, h)]
            hc = slice(h * P, (h + 1) * P)
            for g in passes:
                nc.tensor.matmul_mx(
                    out=acc[:],
                    lhsT=wc[:, g, hc].bitcast(FP8X4),
                    lhsT_scale=ws[:, g, hc],
                    rhs=xc[:, g, :].bitcast(FP8X4),
                    rhs_scale=xs[:, g, :],
                    start=(g == 0),
                    stop=(g == PASSES - 1),
                )

        u_tiles = {}

        def products(G, h, lo, hi):
            if G not in u_tiles:
                u_tiles[G] = up.tile([P, 2, 16, 4, 32], F32, name="u", tag="u")
            u = u_tiles[G]
            acc = acc_tiles[(G, h)]
            m = 4 * G + h
            if lo == 0 and hi == 4:
                nc.vector.scalar_tensor_tensor(
                    out=u[:, :, :, h, :],
                    in0=acc[:].rearrange("p (o a r) -> p o a r", o=1, r=32).to_broadcast([P, 2, 16, 32]),
                    scalar=bias[:, m : m + 1],
                    in1=table[:].rearrange("p t b (j r) -> p t (b j) r", r=32),
                    op0=ALU.add, op1=ALU.mult,
                )
            else:
                for tab in range(2):
                    nc.vector.scalar_tensor_tensor(
                        out=u[:, tab, 4 * lo : 4 * hi, h, :],
                        in0=acc[:, P * lo : P * hi].rearrange("p (a r) -> p a r", r=32),
                        scalar=bias[:, m : m + 1],
                        in1=table[:, tab, lo:hi, :].rearrange("p b (j r) -> p (b j) r", r=32),
                        op0=ALU.add, op1=ALU.mult,
                    )
            if hi == 4:
                acc_tiles.pop((G, h))

        def rotate_store(G, b):
            u = u_tiles[G]
            out_m = out_0 if G < 4 else out_1
            scale = 1.0 / math.sqrt(128.0) if G < 4 else 1.0
            h0 = (G % 4) * 4
            tr = accp.tile([P, 512], F32, name="tr", tag="acc")
            for j in range(4):
                a = 4 * b + j
                nc.tensor.matmul(
                    out=tr[:, j * P : (j + 1) * P], lhsT=u[:, 0, a, :, :].rearrange("p h r -> p (h r)"),
                    rhs=ident[:], start=True, stop=False, is_transpose=True,
                )
                nc.tensor.matmul(
                    out=tr[:, j * P : (j + 1) * P], lhsT=u[:, 1, a, :, :].rearrange("p h r -> p (h r)"),
                    rhs=pswap[:], start=False, stop=True, is_transpose=True,
                )
            o = op.tile([P, 512], F32, name="o", tag="o")
            nc.scalar.activation(out=o[:], in_=tr[:], func=ACT.Copy, scale=scale)
            nc.sync.dma_start(
                out=out_m[b, h0 : h0 + 4, :, :].rearrange("h (r j) d -> (h r) (j d)", j=4), in_=o[:]
            )

        for g in range(PASSES):
            turn_x(g)
            if g == 1:
                turn_bias()
            if g >= 1:
                quantize_x(g - 1)
            if g == 2:
                nc.vector.tensor_copy(out=bias[:], in_=bias_ps[:, 0:32])
        make_table()
        for g in range(PASSES):
            for hf in range(2):
                interleave_unit(0, g, [hf], HEAD_SHARE[0][2 * g + hf])
            if g == 0:
                quantize_x(3)
            if g >= 1:
                quantize(0, g - 1, 1)
                for h in range(4):
                    project(0, h, [g - 1])
        quantize(0, 3, 1)
        for h in range(4):
            project(0, h, [3])

        for g in range(PASSES):
            for hf in range(2):
                interleave_unit(1, g, [hf], HEAD_SHARE[1][2 * g + hf])
            if g >= 1:
                quantize(1, g - 1, 1)
                for h in range(4):
                    project(1, h, [g - 1])
            if g == 2:
                products(0, 0, 0, 4)
        quantize(1, 3, 1)
        for h in range(4):
            project(1, h, [3])

        s_stream = [
            (G, g, hf) for G in range(2, NG) for g in range(PASSES) for hf in range(2) if share_of(G)[2 * g + hf] == "S"
        ]

        def scalar_next():
            if s_stream:
                G, g, hf = s_stream.pop(0)
                interleave_unit(G, g, [hf], "S")

        for i in range(S_LEAD):
            scalar_next()
        for c in range(NG):
            if c + 2 < NG:
                interleave(c + 2, "G")
            if c < NG - 1:
                for h in range(4):
                    if c > 0 or h > 0:
                        products(c, h, 0, 4)
                    if c > 0:
                        project(c + 1, h, range(PASSES))
                for b in range(4):
                    rotate_store(c, b)
                    scalar_next()
            else:
                for half in range(2):
                    for h in range(4):
                        products(c, h, 2 * half, 2 * half + 2)
                    for b in range(2 * half, 2 * half + 2):
                        rotate_store(c, b)
            if c + 2 < NG:
                interleave(c + 2, "V")
                quantize(c + 2, 0, 1)
                quantize(c + 2, 1, 1)
                quantize(c + 2, 2, 2)
